import numpy as np
import ml_dtypes


def mxq(x, axis, fmt="e4m3"):
    dtype, down = {"e4m3": (ml_dtypes.float8_e4m3fn, 7), "e5m2": (ml_dtypes.float8_e5m2, 14)}[fmt]
    v = np.moveaxis(np.asarray(x, np.float32).astype(ml_dtypes.bfloat16).astype(np.float64), axis, -1)
    blocks = v.reshape(v.shape[:-1] + (-1, 32))
    amax = np.abs(blocks).max(-1, keepdims=True)
    byte = np.maximum(np.where(amax > 0, np.frexp(amax)[1] - 1 + 127, 0) - down, 1)
    scale = np.exp2(byte - 127.0)
    codes = (blocks / scale).astype(np.float32).astype(dtype).astype(np.float64)
    return np.moveaxis((codes * scale).reshape(v.shape), -1, axis)


WIDE = False


def mx_kscale(k):
    if not WIDE:
        return np.ones(k)
    levels = np.array([30, -30])
    if k % 512:
        return np.exp2(np.random.permutation(np.resize(levels, k // 32))).repeat(32)
    a = np.empty((k // 512, 16))
    for p in range(k // 512):
        a[p, :8] = np.random.permutation(np.resize(levels, 8))
        for g in range(8):
            far = levels[np.abs(levels - a[p, g]) >= 10]
            a[p, g + 8] = far[np.random.randint(len(far))]
    return np.exp2(a.ravel()).repeat(32)


BF16 = ml_dtypes.bfloat16


def bf(x):
    return np.asarray(x, np.float32).astype(BF16)


def f64(x):
    return np.asarray(x).astype(np.float64)


B, S, D, H, KVH, HD = 1, 512, 2048, 16, 4, 128
E = H * HD
KV = KVH * HD
EPS = 1e-6


def layernorm(u, gamma, beta):
    mu = u.mean(-1, keepdims=True)
    var = np.square(u - mu).mean(-1, keepdims=True)
    return (u - mu) / np.sqrt(var + EPS) * gamma + beta


def apply_rope(u, cos, sin):
    half = u.shape[-1] // 2
    rotated = np.concatenate([-u[..., half:], u[..., :half]], axis=-1)
    return u * cos[None, None] + rotated * sin[None, None]


def setup_inputs():
    s = mx_kscale(D)
    return {
        "x": bf(np.random.standard_normal((B, S, D)) * s),
        "cos": bf(np.random.uniform(size=(S, HD))),
        "sin": bf(np.random.uniform(size=(S, HD))),
        "Wq": bf(np.random.standard_normal((D, E)) / np.sqrt(D) / s[:, None]),
        "Wk": bf(np.random.standard_normal((D, KV)) / np.sqrt(D) / s[:, None]),
        "Wv": bf(np.random.standard_normal((D, KV)) * 2.0 / np.sqrt(D) / s[:, None]),
        "q_gamma": bf(1.0 + 0.1 * np.random.standard_normal(HD)),
        "q_beta": bf(0.1 * np.random.standard_normal(HD)),
        "k_gamma": bf(1.0 + 0.1 * np.random.standard_normal(HD)),
        "k_beta": bf(0.1 * np.random.standard_normal(HD)),
    }


def reference(x, cos, sin, Wq, Wk, Wv, q_gamma, q_beta, k_gamma, k_beta):
    xq = mxq(f64(x), 2, "e5m2")
    q = (xq @ mxq(f64(Wq), 0, "e4m3")).reshape(B, S, H, HD).transpose(0, 2, 1, 3)
    k = (xq @ mxq(f64(Wk), 0, "e4m3")).reshape(B, S, KVH, HD).transpose(0, 2, 1, 3)
    v = (xq @ mxq(f64(Wv), 0, "e4m3")).reshape(B, S, KVH, HD).transpose(0, 2, 1, 3)
    q = layernorm(q, f64(q_gamma), f64(q_beta))
    k = layernorm(k, f64(k_gamma), f64(k_beta))
    q_rot = apply_rope(q, f64(cos), f64(sin))
    k_rot = apply_rope(k, f64(cos), f64(sin))
    return q_rot, k_rot, v

@@ -1,0 +1,284 @@
+from contextlib import ExitStack
+
+import concourse.mybir as mybir
+from concourse.masks import make_identity
+
+S, D, HD = 512, 2048, 128
+H, KVH = 16, 4
+EPS = 1e-6
+FLOPS = 2 * S * D * (H + 2 * KVH) * HD
+
+F32 = mybir.dt.float32
+BF16 = mybir.dt.bfloat16
+U32 = mybir.dt.uint32
+U8 = mybir.dt.uint8
+E4M3 = mybir.dt.float8_e4m3fn_x4
+E5M2 = mybir.dt.float8_e5m2_x4
+ALU = mybir.AluOpType
+ACT = mybir.ActivationFunctionType
+
+P = 128
+PACK = 4
+K_PASS = P * PACK
+PASSES = D // K_PASS
+TT = S // P
+NB = 512
+HB = NB // HD
+HALF = HD // 2
+
+
+def tile_gqa_flashattn_pa_kernel(
+    tc, x, cos, sin, Wq, Wk, Wv, q_gamma, q_beta, k_gamma, k_beta, out_0, out_1, out_2
+):
+    nc = tc.nc
+    blocks = [(Wk, 0, out_1, 0)] + [(Wq, b * NB, out_0, b * HB) for b in range(H // HB)] + [(Wv, 0, out_2, 0)]
+    n_blocks = len(blocks)
+    v_block = n_blocks - 1
+    n_units = v_block * TT
+
+    with ExitStack() as ctx:
+        keep = ctx.enter_context(tc.tile_pool(name="keep", bufs=1))
+        work = ctx.enter_context(tc.tile_pool(name="work", bufs=1))
+        psum = ctx.enter_context(tc.psum_pool(name="psum", bufs=8))
+        ctx.enter_context(tc.manual_schedule())
+
+        ident = keep.tile([P, P], F32, name="ident")
+        make_identity(nc, ident[:])
+        ones = keep.tile([P, P], BF16, name="ones")
+        vec_rows = keep.tile([P, 4, HD], BF16, name="vec_rows")
+        nc.vector.memset(vec_rows[:], 0.0)
+        nc.vector.memset(ones[:], 1.0)
+        for i, vec in enumerate((q_gamma, q_beta, k_gamma, k_beta)):
+            nc.scalar.dma_start(out=vec_rows[0:1, i, :], in_=vec.unsqueeze(0))
+
+        cs = keep.tile([P, TT, 2, HD], BF16, name="cs")
+        sin_sb = keep.tile([P, TT, HD], BF16, name="sin_sb")
+        x_rows = x[0].rearrange("(p t) k -> p t k", t=TT)
+        x_raw = {}
+        w_raw = {}
+
+        def load_x(t):
+            x_raw[t] = keep.tile([P, D], BF16, name="x_raw%d" % t)
+            nc.sync.dma_start(out=x_raw[t][:], in_=x_rows[:, t, :])
+
+        def load_w(b, g):
+            w, col0 = blocks[b][0], blocks[b][1]
+            w_raw[b, g] = work.tile([P, PACK, NB], BF16, name="w_raw", bufs=20)
+            rows = w[g * K_PASS : (g + 1) * K_PASS, col0 : col0 + NB]
+            nc.sync.dma_start(out=w_raw[b, g][:], in_=rows.rearrange("(p j) n -> p j n", j=PACK))
+
+        nc.sync.dma_start(out=sin_sb[:], in_=sin.rearrange("(p t) c -> p t c", t=TT))
+        nc.sync.dma_start(out=cs[:, :, 0, :], in_=cos.rearrange("(p t) c -> p t c", t=TT))
+        load_x(0)
+        for g in range(PASSES):
+            load_w(0, g)
+        for t in range(1, TT):
+            load_x(t)
+        for b in range(1, n_blocks):
+            for g in range(PASSES):
+                load_w(b, g)
+
+        x_grouped, x_codes, x_scales = {}, {}, {}
+        w_grouped, w_codes, w_scales = {}, {}, {}
+        acc, stats, rstd, prods, sums, stage = {}, {}, {}, {}, {}, {}
+
+        def transpose_x(t):
+            words = x_raw[t][:].bitcast(F32)
+            x_grouped[t] = work.tile([P, PASSES, P, PACK], BF16, name="x_grouped", bufs=2, align_bytes=64)
+            for g0 in range(0, PASSES, 2):
+                bank = psum.tile([P, 2, 2, P], F32, name="bank")
+                for g in range(2):
+                    for u in range(2):
+                        w0 = 256 * (g0 + g)
+                        nc.tensor.transpose(bank[:, g, u, :], words[:, w0 + u : w0 + 256 : 2], ident[:])
+                dst = x_grouped[t][:, g0 : g0 + 2, :, :].rearrange("p g r j -> p (g r j)").bitcast(F32)
+                nc.scalar.copy(
+                    out=dst.rearrange("p (g r u) -> p g r u", g=2, u=2),
+                    in_=bank[:].rearrange("p g u r -> p g r u"),
+                )
+
+        def quantize_x(t):
+            x_codes[t] = keep.tile([P, PASSES, P], U32, name="x_codes%d" % t, align_bytes=64)
+            x_scales[t] = keep.tile([P, PASSES, P], U8, name="x_scales%d" % t, align_bytes=64)
+            nc.vector.quantize_mx(
+                out=x_codes[t][:].rearrange("p g r -> p (g r)").bitcast(E5M2),
+                scales=x_scales[t][:].rearrange("p g r -> p (g r)"),
+                in_=x_grouped[t][:].rearrange("p g r j -> p (g r j)"),
+            )
+
+        def interleave_w(b, g, copy):
+            w_grouped[b, g] = work.tile([P, NB, PACK], BF16, name="w_grouped", bufs=4, align_bytes=64)
+            copy(
+                out=w_grouped[b, g][:].rearrange("p (c i) j -> p c j i", i=4),
+                in_=w_raw[b, g][:].rearrange("p j (c i) -> p c j i", i=4),
+            )
+
+        def quantize_w(b, g):
+            w_codes[b, g] = work.tile([P, NB], U32, name="w_codes", bufs=9, align_bytes=64)
+            w_scales[b, g] = work.tile([P, NB], U8, name="w_scales", bufs=9, align_bytes=64)
+            nc.vector.quantize_mx(
+                out=w_codes[b, g][:].bitcast(E4M3),
+                scales=w_scales[b, g][:],
+                in_=w_grouped[b, g][:].rearrange("p n j -> p (n j)"),
+            )
+
+        def mx_pass(b, t, g):
+            if g == 0:
+                acc[b, t] = psum.tile([P, HB, HD], F32, name="bank")
+            nc.tensor.matmul_mx(
+                out=acc[b, t][:].rearrange("p h c -> p (h c)"),
+                lhsT=x_codes[t][:, g, :].bitcast(E5M2),
+                lhsT_scale=x_scales[t][:, g, :],
+                rhs=w_codes[b, g][:].bitcast(E4M3),
+                rhs_scale=w_scales[b, g][:],
+                start=(g == 0),
+                stop=(g == PASSES - 1),
+            )
+
+        def add_rotated(engine, dst, src):
+            engine.tensor_tensor(out=dst[:, :, 0:HALF], in0=src[:, :, 0, 0:HALF], in1=src[:, :, 1, HALF:HD], op=ALU.add)
+            engine.tensor_tensor(out=dst[:, :, HALF:HD], in0=src[:, :, 0, HALF:HD], in1=src[:, :, 1, 0:HALF], op=ALU.add)
+
+        def times_tables(engine, dst, vec):
+            engine.tensor_tensor(
+                out=dst[:].rearrange("p t r c -> p (t r) c"),
+                in0=vec.unsqueeze(1).to_broadcast([P, 2 * TT, HD]),
+                in1=cs[:].rearrange("p t r c -> p (t r) c"),
+                op=ALU.mult,
+            )
+
+        def norm_and_products(b, t):
+            bank = acc[b, t]
+            stats[b, t] = work.tile([P, HB, 3], F32, name="stats", bufs=3)
+            for h in range(0, HB, 2):
+                nc.vector.bn_stats(
+                    out=stats[b, t][:, h : h + 2, :].rearrange("p h s -> p (h s)"),
+                    in_=bank[:, h : h + 2, :].rearrange("p h c -> p c h"),
+                )
+            prods[b, t] = work.tile([P, HB, 2, HD], F32, name="prods", bufs=3)
+            gain = k_gain if b == 0 else q_gain
+            for h in range(HB):
+                nc.vector.scalar_tensor_tensor(
+                    out=prods[b, t][:, h, :, :],
+                    in0=bank[:, h, :].unsqueeze(1).to_broadcast([P, 2, HD]),
+                    scalar=stats[b, t][:, h, 1:2],
+                    in1=gain[:, t, :, :],
+                    op0=ALU.subtract,
+                    op1=ALU.mult,
+                )
+
+        def inverse_std(b, t):
+            rstd[b, t] = work.tile([P, HB], F32, name="rstd", bufs=3)
+            nc.scalar.activation(
+                out=rstd[b, t][:], in_=stats[b, t][:, :, 2], func=ACT.Abs_reciprocal_sqrt, scale=1.0 / HD, bias=EPS
+            )
+
+        def sum_products(b, t):
+            sums[b, t] = work.tile([P, HB, HD], F32, name="sums", bufs=1)
+            add_rotated(nc.gpsimd, sums[b, t], prods[b, t])
+
+        def stage_of(b):
+            if b not in stage:
+                stage[b] = work.tile([P, HB, TT, HD], F32, name="stage", bufs=3)
+            return stage[b]
+
+        def store_head(b, h):
+            out, head0 = blocks[b][2], blocks[b][3]
+            nc.sync.dma_start(out=out[0, head0 + h].rearrange("(p t) c -> p t c", t=TT), in_=stage[b][:, h, :, :])
+
+        def finish(b, t):
+            shift = k_shift if b == 0 else q_shift
+            for h in range(HB):
+                nc.vector.scalar_tensor_tensor(
+                    out=stage_of(b)[:, h, t, :],
+                    in0=sums[b, t][:, h, :],
+                    scalar=rstd[b, t][:, h : h + 1],
+                    in1=shift[:, t, :],
+                    op0=ALU.mult,
+                    op1=ALU.add,
+                )
+                if t == TT - 1:
+                    store_head(b, h)
+
+        vecs = psum.tile([P, 4, HD], F32, name="bank")
+        nc.tensor.matmul(
+            vecs[:].rearrange("p v c -> p (v c)"), lhsT=ones[:], rhs=vec_rows[:].rearrange("p v c -> p (v c)"), start=True, stop=True
+        )
+        q_gamma_sb = keep.tile([P, HD], F32, name="q_gamma_sb")
+        nc.scalar.copy(out=q_gamma_sb[:], in_=vecs[:, 0, :])
+        nc.vector.tensor_copy(out=cs[:, :, 1, 0:HALF], in_=sin_sb[:, :, HALF:HD])
+        nc.vector.tensor_scalar(out=cs[:, :, 1, HALF:HD], in0=sin_sb[:, :, 0:HALF], scalar1=-1.0, scalar2=None, op0=ALU.mult)
+        q_gain = keep.tile([P, TT, 2, HD], F32, name="q_gain")
+        k_gain = keep.tile([P, TT, 2, HD], F32, name="k_gain")
+        q_shift = keep.tile([P, TT, HD], F32, name="q_shift")
+        k_shift = keep.tile([P, TT, HD], F32, name="k_shift")
+        q_beta_prods = work.tile([P, TT, 2, HD], F32, name="prods", bufs=3)
+        k_beta_prods = work.tile([P, TT, 2, HD], F32, name="prods", bufs=3)
+        times_tables(nc.gpsimd, q_gain, q_gamma_sb[:])
+        times_tables(nc.vector, k_beta_prods, vecs[:, 3, :])
+        times_tables(nc.vector, k_gain, vecs[:, 2, :])
+        times_tables(nc.vector, q_beta_prods, vecs[:, 1, :])
+        add_rotated(nc.vector, k_shift, k_beta_prods)
+
+        transpose_x(0)
+        interleave_w(0, 0, nc.scalar.copy)
+        quantize_x(0)
+        interleave_w(0, 1, nc.vector.tensor_copy)
+        interleave_w(0, 2, nc.scalar.copy)
+        quantize_w(0, 0)
+        quantize_w(0, 1)
+        mx_pass(0, 0, 0)
+        mx_pass(0, 0, 1)
+        transpose_x(1)
+        interleave_w(0, 3, nc.vector.tensor_copy)
+        quantize_w(0, 2)
+        quantize_w(0, 3)
+        mx_pass(0, 0, 2)
+        mx_pass(0, 0, 3)
+        add_rotated(nc.vector, q_shift, q_beta_prods)
+        quantize_x(1)
+        transpose_x(2)
+
+        due = {c: [] for c in range(n_units + 1)}
+        for b in range(1, n_blocks):
+            for g in range(PASSES):
+                c = TT * (b - 1) + g
+                if b == 1 and g < 2:
+                    c += 1
+                due[c].append((b, g))
+
+        for c in range(n_units):
+            b, t = divmod(c, TT)
+            if c > 0:
+                sum_products(*divmod(c - 1, TT))
+            if b == 0 and t + 1 < TT:
+                for g in range(PASSES):
+                    mx_pass(0, t + 1, g)
+            if c == 0:
+                transpose_x(3)
+            for wb, wg in due[c + 1]:
+                interleave_w(wb, wg, nc.scalar.copy)
+            norm_and_products(b, t)
+            inverse_std(b, t)
+            if b == 0 and t + 2 < TT:
+                quantize_x(t + 2)
+            for wb, wg in due[c]:
+                quantize_w(wb, wg)
+                if wb == v_block:
+                    for vt in range(TT):
+                        mx_pass(wb, vt, wg)
+            if t == TT - 1 and b + 1 < v_block:
+                for nt in range(TT):
+                    for g in range(PASSES):
+                        mx_pass(b + 1, nt, g)
+            if c > 0:
+                finish(*divmod(c - 1, TT))
+
+        last = divmod(n_units - 1, TT)
+        sum_products(*last)
+        for t in range(TT):
+            copy = nc.scalar.copy if t % 2 == 0 else nc.vector.tensor_copy
+            copy(out=stage_of(v_block)[:, :, t, :], in_=acc[v_block, t][:])
+        finish(*last)
+        for h in range(HB):
+            store_head(v_block, h)

@@ -25,6 +25,7 @@ TT = S // P
 NB = 512
 HB = NB // HD
 HALF = HD // 2
+V_COLS = 192
 
 
 def tile_gqa_flashattn_pa_kernel(
@@ -44,12 +45,18 @@ def tile_gqa_flashattn_pa_kernel(
 
         ident = keep.tile([P, P], F32, name="ident")
         make_identity(nc, ident[:])
-        ones = keep.tile([P, P], BF16, name="ones")
-        vec_rows = keep.tile([P, 4, HD], BF16, name="vec_rows")
+        ident_bf = keep.tile([P, P], BF16, name="ident_bf")
+        make_identity(nc, ident_bf[:])
+        swap = keep.tile([P, P], F32, name="swap")
+        nc.gpsimd.tensor_copy(out=swap[:, 0:HALF], in_=ident[:, HALF:HD])
+        nc.gpsimd.tensor_copy(out=swap[:, HALF:HD], in_=ident[:, 0:HALF])
+        vec_rows = keep.tile([P, HD], BF16, name="vec_rows")
         nc.vector.memset(vec_rows[:], 0.0)
-        nc.vector.memset(ones[:], 1.0)
-        for i, vec in enumerate((q_gamma, q_beta, k_gamma, k_beta)):
-            nc.scalar.dma_start(out=vec_rows[0:1, i, :], in_=vec.unsqueeze(0))
+        for i, vec in enumerate((q_gamma, k_gamma, q_beta, k_beta)):
+            nc.scalar.dma_start(out=vec_rows[i : i + 1, :], in_=vec.unsqueeze(0))
+        for i, vec in enumerate((q_beta, k_beta)):
+            nc.scalar.dma_start(out=vec_rows[4 + i : 5 + i, 0:HALF], in_=vec[HALF:HD].unsqueeze(0))
+            nc.scalar.dma_start(out=vec_rows[4 + i : 5 + i, HALF:HD], in_=vec[0:HALF].unsqueeze(0))
 
         cs = keep.tile([P, TT, 2, HD], BF16, name="cs")
         sin_sb = keep.tile([P, TT, HD], BF16, name="sin_sb")
@@ -80,7 +87,7 @@ def tile_gqa_flashattn_pa_kernel(
 
         x_grouped, x_codes, x_scales = {}, {}, {}
         w_grouped, w_codes, w_scales = {}, {}, {}
-        acc, stats, rstd, prods, sums, stage = {}, {}, {}, {}, {}, {}
+        acc, stats, rstd, nmr, normed, normed_t, prods, res, stage = {}, {}, {}, {}, {}, {}, {}, {}, {}
 
         def transpose_x(t):
             words = x_raw[t][:].bitcast(F32)
@@ -106,11 +113,12 @@ def tile_gqa_flashattn_pa_kernel(
                 in_=x_grouped[t][:].rearrange("p g r j -> p (g r j)"),
             )
 
-        def interleave_w(b, g, copy):
-            w_grouped[b, g] = work.tile([P, NB, PACK], BF16, name="w_grouped", bufs=4, align_bytes=64)
+        def interleave_w(b, g, copy, n0, n1):
+            if (b, g) not in w_grouped:
+                w_grouped[b, g] = work.tile([P, NB, PACK], BF16, name="w_grouped", bufs=4, align_bytes=64)
             copy(
-                out=w_grouped[b, g][:].rearrange("p (c i) j -> p c j i", i=4),
-                in_=w_raw[b, g][:].rearrange("p j (c i) -> p c j i", i=4),
+                out=w_grouped[b, g][:, n0:n1, :].rearrange("p (c i) j -> p c j i", i=4),
+                in_=w_raw[b, g][:, :, n0:n1].rearrange("p j (c i) -> p c j i", i=4),
             )
 
         def quantize_w(b, g):
@@ -135,36 +143,16 @@ def tile_gqa_flashattn_pa_kernel(
                 stop=(g == PASSES - 1),
             )
 
-        def add_rotated(engine, dst, src):
-            engine.tensor_tensor(out=dst[:, :, 0:HALF], in0=src[:, :, 0, 0:HALF], in1=src[:, :, 1, HALF:HD], op=ALU.add)
-            engine.tensor_tensor(out=dst[:, :, HALF:HD], in0=src[:, :, 0, HALF:HD], in1=src[:, :, 1, 0:HALF], op=ALU.add)
+        def mx_unit(b, t):
+            for g in range(PASSES):
+                mx_pass(b, t, g)
 
-        def times_tables(engine, dst, vec):
-            engine.tensor_tensor(
-                out=dst[:].rearrange("p t r c -> p (t r) c"),
-                in0=vec.unsqueeze(1).to_broadcast([P, 2 * TT, HD]),
-                in1=cs[:].rearrange("p t r c -> p (t r) c"),
-                op=ALU.mult,
-            )
-
-        def norm_and_products(b, t):
-            bank = acc[b, t]
+        def head_stats(b, t):
             stats[b, t] = work.tile([P, HB, 3], F32, name="stats", bufs=3)
             for h in range(0, HB, 2):
                 nc.vector.bn_stats(
                     out=stats[b, t][:, h : h + 2, :].rearrange("p h s -> p (h s)"),
-                    in_=bank[:, h : h + 2, :].rearrange("p h c -> p c h"),
-                )
-            prods[b, t] = work.tile([P, HB, 2, HD], F32, name="prods", bufs=3)
-            gain = k_gain if b == 0 else q_gain
-            for h in range(HB):
-                nc.vector.scalar_tensor_tensor(
-                    out=prods[b, t][:, h, :, :],
-                    in0=bank[:, h, :].unsqueeze(1).to_broadcast([P, 2, HD]),
-                    scalar=stats[b, t][:, h, 1:2],
-                    in1=gain[:, t, :, :],
-                    op0=ALU.subtract,
-                    op1=ALU.mult,
+                    in_=acc[b, t][:, h : h + 2, :].rearrange("p h c -> p c h"),
                 )
 
         def inverse_std(b, t):
@@ -173,9 +161,45 @@ def tile_gqa_flashattn_pa_kernel(
                 out=rstd[b, t][:], in_=stats[b, t][:, :, 2], func=ACT.Abs_reciprocal_sqrt, scale=1.0 / HD, bias=EPS
             )
 
-        def sum_products(b, t):
-            sums[b, t] = work.tile([P, HB, HD], F32, name="sums", bufs=1)
-            add_rotated(nc.gpsimd, sums[b, t], prods[b, t])
+        def norm_bias(b, t):
+            nmr[b, t] = work.tile([P, HB], F32, name="nmr", bufs=3)
+            nc.vector.scalar_tensor_tensor(
+                out=nmr[b, t][:], in0=stats[b, t][:, :, 1], scalar=-1.0, in1=rstd[b, t][:], op0=ALU.mult, op1=ALU.mult
+            )
+
+        def normalize(b, t):
+            normed[b, t] = work.tile([P, HB, HD], F32, name="normed", bufs=3)
+            for h in range(HB):
+                nc.scalar.activation(
+                    out=normed[b, t][:, h, :],
+                    in_=acc[b, t][:, h, :],
+                    func=ACT.Identity,
+                    scale=rstd[b, t][:, h : h + 1],
+                    bias=nmr[b, t][:, h : h + 1],
+                )
+
+        def transpose_normed(b, t):
+            normed_t[b, t] = psum.tile([P, HB, P], F32, name="bank")
+            for h in range(HB):
+                nc.tensor.transpose(normed_t[b, t][:, h, :], normed[b, t][:, h, :], ident[:])
+
+        def products(b, t):
+            prods[b, t] = work.tile([P, HB, 2, P], F32, name="prods", bufs=2)
+            nc.vector.tensor_tensor(
+                out=prods[b, t][:],
+                in0=normed_t[b, t][:].unsqueeze(2).to_broadcast([P, HB, 2, P]),
+                in1=gain[b > 0][:, t, :, :].unsqueeze(1).to_broadcast([P, HB, 2, P]),
+                op=ALU.mult,
+            )
+
+        def sum_back(b, t):
+            res[b, t] = psum.tile([P, HB, HD], F32, name="bank")
+            for h in range(HB):
+                terms = ((shift[b > 0][:, t, :], ident), (prods[b, t][:, h, 0, :], ident), (prods[b, t][:, h, 1, :], swap))
+                for i, (term, perm) in enumerate(terms):
+                    nc.tensor.matmul(
+                        res[b, t][:, h, :], lhsT=term, rhs=perm[:], is_transpose=True, start=(i == 0), stop=(i == 2)
+                    )
 
         def stage_of(b):
             if b not in stage:
@@ -186,99 +210,118 @@ def tile_gqa_flashattn_pa_kernel(
             out, head0 = blocks[b][2], blocks[b][3]
             nc.sync.dma_start(out=out[0, head0 + h].rearrange("(p t) c -> p t c", t=TT), in_=stage[b][:, h, :, :])
 
-        def finish(b, t):
-            shift = k_shift if b == 0 else q_shift
-            for h in range(HB):
-                nc.vector.scalar_tensor_tensor(
-                    out=stage_of(b)[:, h, t, :],
-                    in0=sums[b, t][:, h, :],
-                    scalar=rstd[b, t][:, h : h + 1],
-                    in1=shift[:, t, :],
-                    op0=ALU.mult,
-                    op1=ALU.add,
-                )
-                if t == TT - 1:
+        def copy_out(b, t, bank, copy):
+            copy(out=stage_of(b)[:, :, t, :], in_=bank[:])
+            if t == TT - 1:
+                for h in range(HB):
                     store_head(b, h)
 
-        vecs = psum.tile([P, 4, HD], F32, name="bank")
-        nc.tensor.matmul(
-            vecs[:].rearrange("p v c -> p (v c)"), lhsT=ones[:], rhs=vec_rows[:].rearrange("p v c -> p (v c)"), start=True, stop=True
-        )
-        q_gamma_sb = keep.tile([P, HD], F32, name="q_gamma_sb")
-        nc.scalar.copy(out=q_gamma_sb[:], in_=vecs[:, 0, :])
+        gain, shift = {}, {}
+
+        def build_tables(is_q):
+            c0 = 0 if is_q else 1
+            gain[is_q] = keep.tile([P, TT, 2, P], F32, name="gain%d" % c0)
+            shift[is_q] = keep.tile([P, TT, P], F32, name="shift%d" % c0)
+            beta_cos = work.tile([P, TT, P], F32, name="normed", bufs=3)
+            nc.vector.tensor_scalar(
+                out=beta_cos[:], in0=cs_t[:, :, 0, :], scalar1=cols[:, 2 + c0 : 3 + c0], scalar2=None, op0=ALU.mult
+            )
+            nc.vector.tensor_scalar(
+                out=gain[is_q][:], in0=cs_t[:], scalar1=cols[:, c0 : c0 + 1], scalar2=None, op0=ALU.mult
+            )
+            nc.vector.scalar_tensor_tensor(
+                out=shift[is_q][:], in0=sin_t[:], scalar=cols[:, 4 + c0 : 5 + c0], in1=beta_cos[:], op0=ALU.mult, op1=ALU.add
+            )
+
         nc.vector.tensor_copy(out=cs[:, :, 1, 0:HALF], in_=sin_sb[:, :, HALF:HD])
         nc.vector.tensor_scalar(out=cs[:, :, 1, HALF:HD], in0=sin_sb[:, :, 0:HALF], scalar1=-1.0, scalar2=None, op0=ALU.mult)
-        q_gain = keep.tile([P, TT, 2, HD], F32, name="q_gain")
-        k_gain = keep.tile([P, TT, 2, HD], F32, name="k_gain")
-        q_shift = keep.tile([P, TT, HD], F32, name="q_shift")
-        k_shift = keep.tile([P, TT, HD], F32, name="k_shift")
-        q_beta_prods = work.tile([P, TT, 2, HD], F32, name="prods", bufs=3)
-        k_beta_prods = work.tile([P, TT, 2, HD], F32, name="prods", bufs=3)
-        times_tables(nc.gpsimd, q_gain, q_gamma_sb[:])
-        times_tables(nc.vector, k_beta_prods, vecs[:, 3, :])
-        times_tables(nc.vector, k_gain, vecs[:, 2, :])
-        times_tables(nc.vector, q_beta_prods, vecs[:, 1, :])
-        add_rotated(nc.vector, k_shift, k_beta_prods)
+        sin_bank = psum.tile([P, TT + 1, P], BF16, name="bank")
+        cs_bank = psum.tile([P, TT, 2, P], BF16, name="bank")
+        for t in range(TT):
+            nc.tensor.transpose(sin_bank[:, t, :], sin_sb[:, t, :], ident_bf[:])
+        nc.tensor.transpose(sin_bank[:, TT, :], vec_rows[:], ident_bf[:])
+        for t in range(TT):
+            for r in range(2):
+                nc.tensor.transpose(cs_bank[:, t, r, :], cs[:, t, r, :], ident_bf[:])
+        cols = keep.tile([P, 6], F32, name="cols")
+        sin_t = keep.tile([P, TT, P], BF16, name="sin_t")
+        cs_t = keep.tile([P, TT, 2, P], BF16, name="cs_t")
+        nc.vector.tensor_copy(out=cols[:], in_=sin_bank[:, TT, 0:6])
+        nc.vector.tensor_copy(out=sin_t[:], in_=sin_bank[:, 0:TT, :])
+        nc.vector.tensor_scalar(out=cols[0:HALF, 4:6], in0=cols[0:HALF, 4:6], scalar1=-1.0, scalar2=None, op0=ALU.mult)
+        nc.vector.tensor_copy(out=cs_t[:], in_=cs_bank[:])
+        build_tables(False)
 
         transpose_x(0)
-        interleave_w(0, 0, nc.scalar.copy)
+        interleave_w(0, 0, nc.scalar.copy, 0, NB)
         quantize_x(0)
-        interleave_w(0, 1, nc.vector.tensor_copy)
-        interleave_w(0, 2, nc.scalar.copy)
+        interleave_w(0, 1, nc.vector.tensor_copy, 0, NB)
+        interleave_w(0, 2, nc.scalar.copy, 0, NB)
         quantize_w(0, 0)
         quantize_w(0, 1)
         mx_pass(0, 0, 0)
         mx_pass(0, 0, 1)
         transpose_x(1)
-        interleave_w(0, 3, nc.vector.tensor_copy)
+        interleave_w(0, 3, nc.vector.tensor_copy, 0, NB)
         quantize_w(0, 2)
         quantize_w(0, 3)
         mx_pass(0, 0, 2)
         mx_pass(0, 0, 3)
-        add_rotated(nc.vector, q_shift, q_beta_prods)
         quantize_x(1)
-        transpose_x(2)
 
-        due = {c: [] for c in range(n_units + 1)}
+        to_interleave = {c: [] for c in range(n_units + 3)}
+        to_quantize = {c: [] for c in range(n_units + 3)}
         for b in range(1, n_blocks):
             for g in range(PASSES):
-                c = TT * (b - 1) + g
+                c = TT * (b - 1) - 1 + g
+                v_cols = V_COLS
                 if b == 1 and g < 2:
-                    c += 1
-                due[c].append((b, g))
+                    c, v_cols = g, NB
+                if b == 1 and g == 2:
+                    v_cols = 0
+                to_interleave[c].append((b, g, v_cols))
+                to_quantize[min(c + 1, TT * (b - 1) + 2)].append((b, g))
 
-        for c in range(n_units):
-            b, t = divmod(c, TT)
-            if c > 0:
-                sum_products(*divmod(c - 1, TT))
-            if b == 0 and t + 1 < TT:
-                for g in range(PASSES):
-                    mx_pass(0, t + 1, g)
-            if c == 0:
-                transpose_x(3)
-            for wb, wg in due[c + 1]:
-                interleave_w(wb, wg, nc.scalar.copy)
-            norm_and_products(b, t)
-            inverse_std(b, t)
-            if b == 0 and t + 2 < TT:
-                quantize_x(t + 2)
-            for wb, wg in due[c]:
+        def unit(c):
+            return divmod(c, TT)
+
+        for c in range(n_units + 3):
+            if c + 2 < TT:
+                transpose_x(c + 2)
+            if c + 1 < n_units:
+                mx_unit(*unit(c + 1))
+            elif c + 1 < n_units + 2:
+                mx_unit(v_block, c + 1 - n_units)
+            if c < n_units:
+                head_stats(*unit(c))
+                inverse_std(*unit(c))
+            if 0 <= c - 1 < n_units:
+                transpose_normed(*unit(c - 1))
+            if 0 <= c - 2 < n_units:
+                products(*unit(c - 2))
+                sum_back(*unit(c - 2))
+            if 0 <= c - 3 < n_units:
+                copy_out(*unit(c - 3), res[unit(c - 3)], nc.scalar.copy)
+            if c < n_units:
+                norm_bias(*unit(c))
+            if c + 2 < TT:
+                quantize_x(c + 2)
+            for wb, wg, v_cols in to_interleave[c]:
+                if v_cols > 0:
+                    interleave_w(wb, wg, nc.vector.tensor_copy, 0, v_cols)
+                if v_cols < NB:
+                    interleave_w(wb, wg, nc.scalar.copy, v_cols, NB)
+            if c < n_units:
+                normalize(*unit(c))
+            for wb, wg in to_quantize[c]:
                 quantize_w(wb, wg)
-                if wb == v_block:
-                    for vt in range(TT):
-                        mx_pass(wb, vt, wg)
-            if t == TT - 1 and b + 1 < v_block:
-                for nt in range(TT):
-                    for g in range(PASSES):
-                        mx_pass(b + 1, nt, g)
-            if c > 0:
-                finish(*divmod(c - 1, TT))
-
-        last = divmod(n_units - 1, TT)
-        sum_products(*last)
-        for t in range(TT):
-            copy = nc.scalar.copy if t % 2 == 0 else nc.vector.tensor_copy
-            copy(out=stage_of(v_block)[:, :, t, :], in_=acc[v_block, t][:])
-        finish(*last)
-        for h in range(HB):
-            store_head(v_block, h)
+            if c == 3:
+                build_tables(True)
+            if c == n_units:
+                mx_unit(v_block, 2)
+                mx_unit(v_block, 3)
+                copy_out(v_block, 0, acc[v_block, 0], nc.vector.tensor_copy)
+                copy_out(v_block, 1, acc[v_block, 1], nc.scalar.copy)
+            if c == n_units + 1:
+                copy_out(v_block, 2, acc[v_block, 2], nc.vector.tensor_copy)
+                copy_out(v_block, 3, acc[v_block, 3], nc.vector.tensor_copy)

@@ -25,7 +25,16 @@ TT = S // P
 NB = 512
 HB = NB // HD
 HALF = HD // 2
-V_COLS = 192
+V_COLS = 224
+G_COLS = 0
+Q_TABLES_AT = 4
+HEAD_S = 128
+GB = 3
+NMR_G = 1
+RV = (384, 384, 128, 128)
+TX2 = 1
+GAIN_S = 2
+KT = 0
 
 
 def tile_gqa_flashattn_pa_kernel(
@@ -43,6 +52,8 @@ def tile_gqa_flashattn_pa_kernel(
         psum = ctx.enter_context(tc.psum_pool(name="psum", bufs=8))
         ctx.enter_context(tc.manual_schedule())
 
+        vec_rows = keep.tile([P, 2, HD], BF16, name="vec_rows")
+        nc.gpsimd.memset(vec_rows[:, 0, :], 0.0)
         ident = keep.tile([P, P], F32, name="ident")
         make_identity(nc, ident[:])
         ident_bf = keep.tile([P, P], BF16, name="ident_bf")
@@ -50,13 +61,6 @@ def tile_gqa_flashattn_pa_kernel(
         swap = keep.tile([P, P], F32, name="swap")
         nc.gpsimd.tensor_copy(out=swap[:, 0:HALF], in_=ident[:, HALF:HD])
         nc.gpsimd.tensor_copy(out=swap[:, HALF:HD], in_=ident[:, 0:HALF])
-        vec_rows = keep.tile([P, HD], BF16, name="vec_rows")
-        nc.vector.memset(vec_rows[:], 0.0)
-        for i, vec in enumerate((q_gamma, k_gamma, q_beta, k_beta)):
-            nc.scalar.dma_start(out=vec_rows[i : i + 1, :], in_=vec.unsqueeze(0))
-        for i, vec in enumerate((q_beta, k_beta)):
-            nc.scalar.dma_start(out=vec_rows[4 + i : 5 + i, 0:HALF], in_=vec[HALF:HD].unsqueeze(0))
-            nc.scalar.dma_start(out=vec_rows[4 + i : 5 + i, HALF:HD], in_=vec[0:HALF].unsqueeze(0))
 
         cs = keep.tile([P, TT, 2, HD], BF16, name="cs")
         sin_sb = keep.tile([P, TT, HD], BF16, name="sin_sb")
@@ -74,10 +78,13 @@ def tile_gqa_flashattn_pa_kernel(
             rows = w[g * K_PASS : (g + 1) * K_PASS, col0 : col0 + NB]
             nc.sync.dma_start(out=w_raw[b, g][:], in_=rows.rearrange("(p j) n -> p j n", j=PACK))
 
+        load_x(0)
         nc.sync.dma_start(out=sin_sb[:], in_=sin.rearrange("(p t) c -> p t c", t=TT))
         nc.sync.dma_start(out=cs[:, :, 0, :], in_=cos.rearrange("(p t) c -> p t c", t=TT))
-        load_x(0)
-        for g in range(PASSES):
+        load_w(0, 0)
+        for i, vec in enumerate((q_gamma, k_gamma, q_beta, k_beta)):
+            nc.sync.dma_start(out=vec_rows[i : i + 1, 0, :], in_=vec.unsqueeze(0))
+        for g in range(1, PASSES):
             load_w(0, g)
         for t in range(1, TT):
             load_x(t)
@@ -87,11 +94,11 @@ def tile_gqa_flashattn_pa_kernel(
 
         x_grouped, x_codes, x_scales = {}, {}, {}
         w_grouped, w_codes, w_scales = {}, {}, {}
-        acc, stats, rstd, nmr, normed, normed_t, prods, res, stage = {}, {}, {}, {}, {}, {}, {}, {}, {}
+        acc, stats, rstd, nmr, normed, normed_t, prods, res = {}, {}, {}, {}, {}, {}, {}, {}
 
         def transpose_x(t):
             words = x_raw[t][:].bitcast(F32)
-            x_grouped[t] = work.tile([P, PASSES, P, PACK], BF16, name="x_grouped", bufs=2, align_bytes=64)
+            x_grouped[t] = work.tile([P, PASSES, P, PACK], BF16, name="x_grouped", bufs=3, align_bytes=64)
             for g0 in range(0, PASSES, 2):
                 bank = psum.tile([P, 2, 2, P], F32, name="bank")
                 for g in range(2):
@@ -113,13 +120,22 @@ def tile_gqa_flashattn_pa_kernel(
                 in_=x_grouped[t][:].rearrange("p g r j -> p (g r j)"),
             )
 
-        def interleave_w(b, g, copy, n0, n1):
+        def grouped_of(b, g):
             if (b, g) not in w_grouped:
-                w_grouped[b, g] = work.tile([P, NB, PACK], BF16, name="w_grouped", bufs=4, align_bytes=64)
-            copy(
-                out=w_grouped[b, g][:, n0:n1, :].rearrange("p (c i) j -> p c j i", i=4),
-                in_=w_raw[b, g][:, :, n0:n1].rearrange("p j (c i) -> p c j i", i=4),
-            )
+                tag, bufs = ("w_grouped_head", 4) if b == 0 else ("w_grouped", GB)
+                w_grouped[b, g] = work.tile([P, NB, PACK], BF16, name=tag, bufs=bufs, align_bytes=64)
+            return w_grouped[b, g]
+
+        def interleave_w(b, g, copy, n0, n1):
+            if n1 > n0:
+                copy(
+                    out=grouped_of(b, g)[:, n0:n1, :].rearrange("p (c i) j -> p c j i", i=4),
+                    in_=w_raw[b, g][:, :, n0:n1].rearrange("p j (c i) -> p c j i", i=4),
+                )
+
+        def interleave_w_gpsimd(b, g, n0, n1):
+            if n1 > n0:
+                nc.gpsimd.tensor_copy(out=grouped_of(b, g)[:, n0:n1, :], in_=w_raw[b, g][:, :, n0:n1].rearrange("p j n -> p n j"))
 
         def quantize_w(b, g):
             w_codes[b, g] = work.tile([P, NB], U32, name="w_codes", bufs=9, align_bytes=64)
@@ -162,10 +178,14 @@ def tile_gqa_flashattn_pa_kernel(
             )
 
         def norm_bias(b, t):
+            neg_mean = work.tile([P, HB], F32, name="neg_mean", bufs=3)
             nmr[b, t] = work.tile([P, HB], F32, name="nmr", bufs=3)
-            nc.vector.scalar_tensor_tensor(
-                out=nmr[b, t][:], in0=stats[b, t][:, :, 1], scalar=-1.0, in1=rstd[b, t][:], op0=ALU.mult, op1=ALU.mult
+            if not NMR_G:
+                return nc.vector.scalar_tensor_tensor(out=nmr[b, t][:], in0=stats[b, t][:, :, 1], scalar=-1.0, in1=rstd[b, t][:], op0=ALU.mult, op1=ALU.mult)
+            nc.gpsimd.tensor_scalar(
+                out=neg_mean[:], in0=stats[b, t][:, :, 1], scalar1=-1.0, scalar2=0.0, op0=ALU.mult, op1=ALU.add
             )
+            nc.gpsimd.tensor_tensor(out=nmr[b, t][:], in0=neg_mean[:], in1=rstd[b, t][:], op=ALU.mult)
 
         def normalize(b, t):
             normed[b, t] = work.tile([P, HB, HD], F32, name="normed", bufs=3)
@@ -201,20 +221,12 @@ def tile_gqa_flashattn_pa_kernel(
                         res[b, t][:, h, :], lhsT=term, rhs=perm[:], is_transpose=True, start=(i == 0), stop=(i == 2)
                     )
 
-        def stage_of(b):
-            if b not in stage:
-                stage[b] = work.tile([P, HB, TT, HD], F32, name="stage", bufs=3)
-            return stage[b]
-
-        def store_head(b, h):
-            out, head0 = blocks[b][2], blocks[b][3]
-            nc.sync.dma_start(out=out[0, head0 + h].rearrange("(p t) c -> p t c", t=TT), in_=stage[b][:, h, :, :])
-
         def copy_out(b, t, bank, copy):
-            copy(out=stage_of(b)[:, :, t, :], in_=bank[:])
-            if t == TT - 1:
-                for h in range(HB):
-                    store_head(b, h)
+            out, head0 = blocks[b][2], blocks[b][3]
+            stage = work.tile([P, HB, HD], F32, name="stage", bufs=6)
+            copy(out=stage[:], in_=bank[:])
+            rows = out[0, head0 : head0 + HB].rearrange("h (p t) c -> p h t c", t=TT)
+            nc.sync.dma_start(out=rows[:, :, t, :], in_=stage[:])
 
         gain, shift = {}, {}
 
@@ -226,102 +238,111 @@ def tile_gqa_flashattn_pa_kernel(
             nc.vector.tensor_scalar(
                 out=beta_cos[:], in0=cs_t[:, :, 0, :], scalar1=cols[:, 2 + c0 : 3 + c0], scalar2=None, op0=ALU.mult
             )
-            nc.vector.tensor_scalar(
-                out=gain[is_q][:], in0=cs_t[:], scalar1=cols[:, c0 : c0 + 1], scalar2=None, op0=ALU.mult
-            )
+            if GAIN_S & (2 if is_q else 1):
+                nc.scalar.activation(out=gain[is_q][:], in_=cs_t[:], func=ACT.Identity, scale=cols[:, c0 : c0 + 1])
+            else:
+                nc.vector.tensor_scalar(
+                    out=gain[is_q][:], in0=cs_t[:], scalar1=cols[:, c0 : c0 + 1], scalar2=None, op0=ALU.mult
+                )
             nc.vector.scalar_tensor_tensor(
-                out=shift[is_q][:], in0=sin_t[:], scalar=cols[:, 4 + c0 : 5 + c0], in1=beta_cos[:], op0=ALU.mult, op1=ALU.add
+                out=shift[is_q][:], in0=sin_t[:], scalar=cols[:, 6 + c0 : 7 + c0], in1=beta_cos[:], op0=ALU.mult, op1=ALU.add
             )
 
+        transpose_x(0)
         nc.vector.tensor_copy(out=cs[:, :, 1, 0:HALF], in_=sin_sb[:, :, HALF:HD])
         nc.vector.tensor_scalar(out=cs[:, :, 1, HALF:HD], in0=sin_sb[:, :, 0:HALF], scalar1=-1.0, scalar2=None, op0=ALU.mult)
-        sin_bank = psum.tile([P, TT + 1, P], BF16, name="bank")
+        nc.vector.tensor_scalar(out=vec_rows[:, 1, 0:HALF], in0=vec_rows[:, 0, HALF:HD], scalar1=-1.0, scalar2=None, op0=ALU.mult)
+        nc.vector.tensor_copy(out=vec_rows[:, 1, HALF:HD], in_=vec_rows[:, 0, 0:HALF])
         cs_bank = psum.tile([P, TT, 2, P], BF16, name="bank")
-        for t in range(TT):
-            nc.tensor.transpose(sin_bank[:, t, :], sin_sb[:, t, :], ident_bf[:])
-        nc.tensor.transpose(sin_bank[:, TT, :], vec_rows[:], ident_bf[:])
+        sin_bank = psum.tile([P, TT + 2, P], BF16, name="bank")
         for t in range(TT):
             for r in range(2):
                 nc.tensor.transpose(cs_bank[:, t, r, :], cs[:, t, r, :], ident_bf[:])
-        cols = keep.tile([P, 6], F32, name="cols")
+        for t in range(TT):
+            nc.tensor.transpose(sin_bank[:, t, :], sin_sb[:, t, :], ident_bf[:])
+        for r in range(2):
+            nc.tensor.transpose(sin_bank[:, TT + r, :], vec_rows[:, r, :], ident_bf[:])
+        cols3 = keep.tile([P, 2, 4], F32, name="cols")
+        cols = cols3[:].rearrange("p r v -> p (r v)")
         sin_t = keep.tile([P, TT, P], BF16, name="sin_t")
         cs_t = keep.tile([P, TT, 2, P], BF16, name="cs_t")
-        nc.vector.tensor_copy(out=cols[:], in_=sin_bank[:, TT, 0:6])
-        nc.vector.tensor_copy(out=sin_t[:], in_=sin_bank[:, 0:TT, :])
-        nc.vector.tensor_scalar(out=cols[0:HALF, 4:6], in0=cols[0:HALF, 4:6], scalar1=-1.0, scalar2=None, op0=ALU.mult)
         nc.vector.tensor_copy(out=cs_t[:], in_=cs_bank[:])
-        build_tables(False)
+        nc.vector.tensor_copy(out=sin_t[:], in_=sin_bank[:, 0:TT, :])
+        nc.vector.tensor_copy(out=cols3[:], in_=sin_bank[:, TT : TT + 2, 0:4])
 
-        transpose_x(0)
         interleave_w(0, 0, nc.scalar.copy, 0, NB)
         quantize_x(0)
         interleave_w(0, 1, nc.vector.tensor_copy, 0, NB)
         interleave_w(0, 2, nc.scalar.copy, 0, NB)
         quantize_w(0, 0)
         quantize_w(0, 1)
-        mx_pass(0, 0, 0)
-        mx_pass(0, 0, 1)
+        interleave_w(0, 3, nc.scalar.copy, 0, HEAD_S)
+        interleave_w(0, 3, nc.vector.tensor_copy, HEAD_S, NB)
         transpose_x(1)
-        interleave_w(0, 3, nc.vector.tensor_copy, 0, NB)
         quantize_w(0, 2)
         quantize_w(0, 3)
-        mx_pass(0, 0, 2)
-        mx_pass(0, 0, 3)
+        if TX2:
+            transpose_x(2)
+        mx_unit(0, 0)
+        if not TX2:
+            transpose_x(2)
         quantize_x(1)
+        transpose_x(3)
 
         to_interleave = {c: [] for c in range(n_units + 3)}
         to_quantize = {c: [] for c in range(n_units + 3)}
         for b in range(1, n_blocks):
             for g in range(PASSES):
-                c = TT * (b - 1) - 1 + g
-                v_cols = V_COLS
-                if b == 1 and g < 2:
-                    c, v_cols = g, NB
-                if b == 1 and g == 2:
-                    v_cols = 0
-                to_interleave[c].append((b, g, v_cols))
+                c, v_cols, g_cols = TT * (b - 1) - 1 + g, V_COLS, G_COLS
+                if b == 1:
+                    c, v_cols, g_cols = (g + 1) // 2, RV[g], 0
+                to_interleave[c].append((b, g, v_cols, g_cols))
                 to_quantize[min(c + 1, TT * (b - 1) + 2)].append((b, g))
 
         def unit(c):
             return divmod(c, TT)
 
         for c in range(n_units + 3):
-            if c + 2 < TT:
-                transpose_x(c + 2)
             if c + 1 < n_units:
                 mx_unit(*unit(c + 1))
-            elif c + 1 < n_units + 2:
-                mx_unit(v_block, c + 1 - n_units)
+            elif c + 1 == n_units:
+                mx_unit(v_block, 0)
+            for wb, wg, v_cols, g_cols in to_interleave[c]:
+                interleave_w_gpsimd(wb, wg, NB - g_cols, NB)
             if c < n_units:
                 head_stats(*unit(c))
                 inverse_std(*unit(c))
+                if NMR_G:
+                    norm_bias(*unit(c))
             if 0 <= c - 1 < n_units:
                 transpose_normed(*unit(c - 1))
+            if c + 1 == n_units:
+                mx_unit(v_block, 1)
             if 0 <= c - 2 < n_units:
                 products(*unit(c - 2))
                 sum_back(*unit(c - 2))
-            if 0 <= c - 3 < n_units:
-                copy_out(*unit(c - 3), res[unit(c - 3)], nc.scalar.copy)
-            if c < n_units:
-                norm_bias(*unit(c))
+            if n_units <= c < n_units + 2:
+                mx_unit(v_block, c - n_units + 2)
             if c + 2 < TT:
                 quantize_x(c + 2)
-            for wb, wg, v_cols in to_interleave[c]:
-                if v_cols > 0:
-                    interleave_w(wb, wg, nc.vector.tensor_copy, 0, v_cols)
-                if v_cols < NB:
-                    interleave_w(wb, wg, nc.scalar.copy, v_cols, NB)
-            if c < n_units:
+            if c == KT:
+                build_tables(False)
+            if c < n_units and not NMR_G:
+                norm_bias(*unit(c))
+            for wb, wg, v_cols, g_cols in to_interleave[c]:
+                interleave_w(wb, wg, nc.vector.tensor_copy, 0, v_cols)
+                interleave_w(wb, wg, nc.scalar.copy, v_cols, NB - g_cols)
+            if c == n_units - 1:
+                normalize(*unit(c))
+            if 0 <= c - 3 < n_units:
+                copy_out(*unit(c - 3), res[unit(c - 3)], nc.scalar.copy)
+            if c < n_units - 1:
                 normalize(*unit(c))
             for wb, wg in to_quantize[c]:
                 quantize_w(wb, wg)
-            if c == 3:
+            if c == Q_TABLES_AT:
                 build_tables(True)
-            if c == n_units:
-                mx_unit(v_block, 2)
-                mx_unit(v_block, 3)
-                copy_out(v_block, 0, acc[v_block, 0], nc.vector.tensor_copy)
-                copy_out(v_block, 1, acc[v_block, 1], nc.scalar.copy)
-            if c == n_units + 1:
-                copy_out(v_block, 2, acc[v_block, 2], nc.vector.tensor_copy)
-                copy_out(v_block, 3, acc[v_block, 3], nc.vector.tensor_copy)
+            if c == n_units - 1:
+                copy_out(v_block, 0, acc[v_block, 0], nc.scalar.copy)
+            if c >= n_units:
+                copy_out(v_block, c - n_units + 1, acc[v_block, c - n_units + 1], nc.vector.tensor_copy)

@@ -25,16 +25,21 @@ TT = S // P
 NB = 512
 HB = NB // HD
 HALF = HD // 2
-V_COLS = 224
-G_COLS = 0
-Q_TABLES_AT = 4
+V_COLS = 32
+G_COLS = 256
+Q_TABLES_AT = -2
 HEAD_S = 128
-GB = 3
-NMR_G = 1
-RV = (384, 384, 128, 128)
+GB = 2
+G_FROM = 2
+V_NOG = 160
+NMR_G = 0
+RV = (256, 384, 128, 128)
 TX2 = 1
-GAIN_S = 2
-KT = 0
+GAIN_S = 0
+KT = -1
+XFIRST = 0
+VEARLY = 0
+SPLIT = 1
 
 
 def tile_gqa_flashattn_pa_kernel(
@@ -78,9 +83,12 @@ def tile_gqa_flashattn_pa_kernel(
             rows = w[g * K_PASS : (g + 1) * K_PASS, col0 : col0 + NB]
             nc.sync.dma_start(out=w_raw[b, g][:], in_=rows.rearrange("(p j) n -> p j n", j=PACK))
 
-        load_x(0)
+        if XFIRST:
+            load_x(0)
         nc.sync.dma_start(out=sin_sb[:], in_=sin.rearrange("(p t) c -> p t c", t=TT))
         nc.sync.dma_start(out=cs[:, :, 0, :], in_=cos.rearrange("(p t) c -> p t c", t=TT))
+        if not XFIRST:
+            load_x(0)
         load_w(0, 0)
         for i, vec in enumerate((q_gamma, k_gamma, q_beta, k_beta)):
             nc.sync.dma_start(out=vec_rows[i : i + 1, 0, :], in_=vec.unsqueeze(0))
@@ -122,7 +130,7 @@ def tile_gqa_flashattn_pa_kernel(
 
         def grouped_of(b, g):
             if (b, g) not in w_grouped:
-                tag, bufs = ("w_grouped_head", 4) if b == 0 else ("w_grouped", GB)
+                tag, bufs = ("w_grouped_head", 4) if b < 2 else ("w_grouped", GB)
                 w_grouped[b, g] = work.tile([P, NB, PACK], BF16, name=tag, bufs=bufs, align_bytes=64)
             return w_grouped[b, g]
 
@@ -146,29 +154,29 @@ def tile_gqa_flashattn_pa_kernel(
                 in_=w_grouped[b, g][:].rearrange("p n j -> p (n j)"),
             )
 
-        def mx_pass(b, t, g):
+        def mx_pass(b, t, g, h0=0, h1=HB):
             if g == 0:
-                acc[b, t] = psum.tile([P, HB, HD], F32, name="bank")
+                acc[b, t, h0] = psum.tile([P, h1 - h0, HD], F32, name="bank")
             nc.tensor.matmul_mx(
-                out=acc[b, t][:].rearrange("p h c -> p (h c)"),
+                out=acc[b, t, h0][:].rearrange("p h c -> p (h c)"),
                 lhsT=x_codes[t][:, g, :].bitcast(E5M2),
                 lhsT_scale=x_scales[t][:, g, :],
-                rhs=w_codes[b, g][:].bitcast(E4M3),
-                rhs_scale=w_scales[b, g][:],
+                rhs=w_codes[b, g][:, h0 * HD : h1 * HD].bitcast(E4M3),
+                rhs_scale=w_scales[b, g][:, h0 * HD : h1 * HD],
                 start=(g == 0),
                 stop=(g == PASSES - 1),
             )
 
-        def mx_unit(b, t):
+        def mx_unit(b, t, h0=0, h1=HB):
             for g in range(PASSES):
-                mx_pass(b, t, g)
+                mx_pass(b, t, g, h0, h1)
 
         def head_stats(b, t):
             stats[b, t] = work.tile([P, HB, 3], F32, name="stats", bufs=3)
             for h in range(0, HB, 2):
                 nc.vector.bn_stats(
                     out=stats[b, t][:, h : h + 2, :].rearrange("p h s -> p (h s)"),
-                    in_=acc[b, t][:, h : h + 2, :].rearrange("p h c -> p c h"),
+                    in_=acc[b, t, 0][:, h : h + 2, :].rearrange("p h c -> p c h"),
                 )
 
         def inverse_std(b, t):
@@ -192,7 +200,7 @@ def tile_gqa_flashattn_pa_kernel(
             for h in range(HB):
                 nc.scalar.activation(
                     out=normed[b, t][:, h, :],
-                    in_=acc[b, t][:, h, :],
+                    in_=acc[b, t, 0][:, h, :],
                     func=ACT.Identity,
                     scale=rstd[b, t][:, h : h + 1],
                     bias=nmr[b, t][:, h : h + 1],
@@ -221,11 +229,11 @@ def tile_gqa_flashattn_pa_kernel(
                         res[b, t][:, h, :], lhsT=term, rhs=perm[:], is_transpose=True, start=(i == 0), stop=(i == 2)
                     )
 
-        def copy_out(b, t, bank, copy):
+        def copy_out(b, t, bank, copy, h0=0, h1=HB):
             out, head0 = blocks[b][2], blocks[b][3]
-            stage = work.tile([P, HB, HD], F32, name="stage", bufs=6)
+            stage = work.tile([P, h1 - h0, HD], F32, name="stage", bufs=6)
             copy(out=stage[:], in_=bank[:])
-            rows = out[0, head0 : head0 + HB].rearrange("h (p t) c -> p h t c", t=TT)
+            rows = out[0, head0 + h0 : head0 + h1].rearrange("h (p t) c -> p h t c", t=TT)
             nc.sync.dma_start(out=rows[:, :, t, :], in_=stage[:])
 
         gain, shift = {}, {}
@@ -248,7 +256,8 @@ def tile_gqa_flashattn_pa_kernel(
                 out=shift[is_q][:], in0=sin_t[:], scalar=cols[:, 6 + c0 : 7 + c0], in1=beta_cos[:], op0=ALU.mult, op1=ALU.add
             )
 
-        transpose_x(0)
+        if XFIRST:
+            transpose_x(0)
         nc.vector.tensor_copy(out=cs[:, :, 1, 0:HALF], in_=sin_sb[:, :, HALF:HD])
         nc.vector.tensor_scalar(out=cs[:, :, 1, HALF:HD], in0=sin_sb[:, :, 0:HALF], scalar1=-1.0, scalar2=None, op0=ALU.mult)
         nc.vector.tensor_scalar(out=vec_rows[:, 1, 0:HALF], in0=vec_rows[:, 0, HALF:HD], scalar1=-1.0, scalar2=None, op0=ALU.mult)
@@ -262,6 +271,8 @@ def tile_gqa_flashattn_pa_kernel(
             nc.tensor.transpose(sin_bank[:, t, :], sin_sb[:, t, :], ident_bf[:])
         for r in range(2):
             nc.tensor.transpose(sin_bank[:, TT + r, :], vec_rows[:, r, :], ident_bf[:])
+        if not XFIRST:
+            transpose_x(0)
         cols3 = keep.tile([P, 2, 4], F32, name="cols")
         cols = cols3[:].rearrange("p r v -> p (r v)")
         sin_t = keep.tile([P, TT, P], BF16, name="sin_t")
@@ -270,6 +281,8 @@ def tile_gqa_flashattn_pa_kernel(
         nc.vector.tensor_copy(out=sin_t[:], in_=sin_bank[:, 0:TT, :])
         nc.vector.tensor_copy(out=cols3[:], in_=sin_bank[:, TT : TT + 2, 0:4])
 
+        if KT == -1:
+            build_tables(False)
         interleave_w(0, 0, nc.scalar.copy, 0, NB)
         quantize_x(0)
         interleave_w(0, 1, nc.vector.tensor_copy, 0, NB)
@@ -281,6 +294,10 @@ def tile_gqa_flashattn_pa_kernel(
         transpose_x(1)
         quantize_w(0, 2)
         quantize_w(0, 3)
+        if KT == -2:
+            build_tables(False)
+        if Q_TABLES_AT == -2:
+            build_tables(True)
         if TX2:
             transpose_x(2)
         mx_unit(0, 0)
@@ -293,7 +310,9 @@ def tile_gqa_flashattn_pa_kernel(
         to_quantize = {c: [] for c in range(n_units + 3)}
         for b in range(1, n_blocks):
             for g in range(PASSES):
-                c, v_cols, g_cols = TT * (b - 1) - 1 + g, V_COLS, G_COLS
+                c, v_cols, g_cols = TT * (b - 1) - 2 + g, V_COLS, G_COLS
+                if b == 2 and g < G_FROM:
+                    v_cols, g_cols = V_NOG, 0
                 if b == 1:
                     c, v_cols, g_cols = (g + 1) // 2, RV[g], 0
                 to_interleave[c].append((b, g, v_cols, g_cols))
@@ -305,8 +324,9 @@ def tile_gqa_flashattn_pa_kernel(
         for c in range(n_units + 3):
             if c + 1 < n_units:
                 mx_unit(*unit(c + 1))
-            elif c + 1 == n_units:
-                mx_unit(v_block, 0)
+            for g in range(PASSES):
+                if min(n_units - 3 + g, n_units - 1) == c if VEARLY else c == n_units - 1:
+                    mx_pass(v_block, 0, g)
             for wb, wg, v_cols, g_cols in to_interleave[c]:
                 interleave_w_gpsimd(wb, wg, NB - g_cols, NB)
             if c < n_units:
@@ -321,8 +341,11 @@ def tile_gqa_flashattn_pa_kernel(
             if 0 <= c - 2 < n_units:
                 products(*unit(c - 2))
                 sum_back(*unit(c - 2))
-            if n_units <= c < n_units + 2:
-                mx_unit(v_block, c - n_units + 2)
+            if c == n_units:
+                mx_unit(v_block, 2)
+            if c == n_units + 1:
+                mx_unit(v_block, 3, 0, HB // 2)
+                mx_unit(v_block, 3, HB // 2, HB)
             if c + 2 < TT:
                 quantize_x(c + 2)
             if c == KT:
@@ -343,6 +366,9 @@ def tile_gqa_flashattn_pa_kernel(
             if c == Q_TABLES_AT:
                 build_tables(True)
             if c == n_units - 1:
-                copy_out(v_block, 0, acc[v_block, 0], nc.scalar.copy)
-            if c >= n_units:
-                copy_out(v_block, c - n_units + 1, acc[v_block, c - n_units + 1], nc.vector.tensor_copy)
+                copy_out(v_block, 0, acc[v_block, 0, 0], nc.scalar.copy)
+            if n_units <= c < n_units + 2:
+                copy_out(v_block, c - n_units + 1, acc[v_block, c - n_units + 1, 0], nc.vector.tensor_copy)
+            if c == n_units + 2:
+                copy_out(v_block, 3, acc[v_block, 3, 0], nc.vector.tensor_copy, 0, HB // 2)
+                copy_out(v_block, 3, acc[v_block, 3, HB // 2], nc.scalar.copy, HB // 2, HB)

from contextlib import ExitStack

import concourse.mybir as mybir
from concourse.masks import make_identity

S, D, HD = 512, 2048, 128
H, KVH = 16, 4
EPS = 1e-6
FLOPS = 2 * S * D * (H + 2 * KVH) * HD

F32 = mybir.dt.float32
BF16 = mybir.dt.bfloat16
U32 = mybir.dt.uint32
U8 = mybir.dt.uint8
E4M3 = mybir.dt.float8_e4m3fn_x4
E5M2 = mybir.dt.float8_e5m2_x4
ALU = mybir.AluOpType
ACT = mybir.ActivationFunctionType

P = 128
PACK = 4
K_PASS = P * PACK
PASSES = D // K_PASS
TT = S // P
NB = 512
HB = NB // HD
HALF = HD // 2
V_COLS = 32
G_COLS = 256
Q_TABLES_AT = -2
HEAD_S = 128
GB = 2
G_FROM = 2
V_NOG = 160
NMR_G = 0
RV = (256, 384, 128, 128)
TX2 = 1
GAIN_S = 0
KT = -1
XFIRST = 0
VEARLY = 0
SPLIT = 1


def tile_gqa_flashattn_pa_kernel(
    tc, x, cos, sin, Wq, Wk, Wv, q_gamma, q_beta, k_gamma, k_beta, out_0, out_1, out_2
):
    nc = tc.nc
    blocks = [(Wk, 0, out_1, 0)] + [(Wq, b * NB, out_0, b * HB) for b in range(H // HB)] + [(Wv, 0, out_2, 0)]
    n_blocks = len(blocks)
    v_block = n_blocks - 1
    n_units = v_block * TT

    with ExitStack() as ctx:
        keep = ctx.enter_context(tc.tile_pool(name="keep", bufs=1))
        work = ctx.enter_context(tc.tile_pool(name="work", bufs=1))
        psum = ctx.enter_context(tc.psum_pool(name="psum", bufs=8))
        ctx.enter_context(tc.manual_schedule())

        vec_rows = keep.tile([P, 2, HD], BF16, name="vec_rows")
        nc.gpsimd.memset(vec_rows[:, 0, :], 0.0)
        ident = keep.tile([P, P], F32, name="ident")
        make_identity(nc, ident[:])
        ident_bf = keep.tile([P, P], BF16, name="ident_bf")
        make_identity(nc, ident_bf[:])
        swap = keep.tile([P, P], F32, name="swap")
        nc.gpsimd.tensor_copy(out=swap[:, 0:HALF], in_=ident[:, HALF:HD])
        nc.gpsimd.tensor_copy(out=swap[:, HALF:HD], in_=ident[:, 0:HALF])

        cs = keep.tile([P, TT, 2, HD], BF16, name="cs")
        sin_sb = keep.tile([P, TT, HD], BF16, name="sin_sb")
        x_rows = x[0].rearrange("(p t) k -> p t k", t=TT)
        x_raw = {}
        w_raw = {}

        def load_x(t):
            x_raw[t] = keep.tile([P, D], BF16, name="x_raw%d" % t)
            nc.sync.dma_start(out=x_raw[t][:], in_=x_rows[:, t, :])

        def load_w(b, g):
            w, col0 = blocks[b][0], blocks[b][1]
            w_raw[b, g] = work.tile([P, PACK, NB], BF16, name="w_raw", bufs=20)
            rows = w[g * K_PASS : (g + 1) * K_PASS, col0 : col0 + NB]
            nc.sync.dma_start(out=w_raw[b, g][:], in_=rows.rearrange("(p j) n -> p j n", j=PACK))

        if XFIRST:
            load_x(0)
        nc.sync.dma_start(out=sin_sb[:], in_=sin.rearrange("(p t) c -> p t c", t=TT))
        nc.sync.dma_start(out=cs[:, :, 0, :], in_=cos.rearrange("(p t) c -> p t c", t=TT))
        if not XFIRST:
            load_x(0)
        load_w(0, 0)
        for i, vec in enumerate((q_gamma, k_gamma, q_beta, k_beta)):
            nc.sync.dma_start(out=vec_rows[i : i + 1, 0, :], in_=vec.unsqueeze(0))
        for g in range(1, PASSES):
            load_w(0, g)
        for t in range(1, TT):
            load_x(t)
        for b in range(1, n_blocks):
            for g in range(PASSES):
                load_w(b, g)

        x_grouped, x_codes, x_scales = {}, {}, {}
        w_grouped, w_codes, w_scales = {}, {}, {}
        acc, stats, rstd, nmr, normed, normed_t, prods, res = {}, {}, {}, {}, {}, {}, {}, {}

        def transpose_x(t):
            words = x_raw[t][:].bitcast(F32)
            x_grouped[t] = work.tile([P, PASSES, P, PACK], BF16, name="x_grouped", bufs=3, align_bytes=64)
            for g0 in range(0, PASSES, 2):
                bank = psum.tile([P, 2, 2, P], F32, name="bank")
                for g in range(2):
                    for u in range(2):
                        w0 = 256 * (g0 + g)
                        nc.tensor.transpose(bank[:, g, u, :], words[:, w0 + u : w0 + 256 : 2], ident[:])
                dst = x_grouped[t][:, g0 : g0 + 2, :, :].rearrange("p g r j -> p (g r j)").bitcast(F32)
                nc.scalar.copy(
                    out=dst.rearrange("p (g r u) -> p g r u", g=2, u=2),
                    in_=bank[:].rearrange("p g u r -> p g r u"),
                )

        def quantize_x(t):
            x_codes[t] = keep.tile([P, PASSES, P], U32, name="x_codes%d" % t, align_bytes=64)
            x_scales[t] = keep.tile([P, PASSES, P], U8, name="x_scales%d" % t, align_bytes=64)
            nc.vector.quantize_mx(
                out=x_codes[t][:].rearrange("p g r -> p (g r)").bitcast(E5M2),
                scales=x_scales[t][:].rearrange("p g r -> p (g r)"),
                in_=x_grouped[t][:].rearrange("p g r j -> p (g r j)"),
            )

        def grouped_of(b, g):
            if (b, g) not in w_grouped:
                tag, bufs = ("w_grouped_head", 4) if b < 2 else ("w_grouped", GB)
                w_grouped[b, g] = work.tile([P, NB, PACK], BF16, name=tag, bufs=bufs, align_bytes=64)
            return w_grouped[b, g]

        def interleave_w(b, g, copy, n0, n1):
            if n1 > n0:
                copy(
                    out=grouped_of(b, g)[:, n0:n1, :].rearrange("p (c i) j -> p c j i", i=4),
                    in_=w_raw[b, g][:, :, n0:n1].rearrange("p j (c i) -> p c j i", i=4),
                )

        def interleave_w_gpsimd(b, g, n0, n1):
            if n1 > n0:
                nc.gpsimd.tensor_copy(out=grouped_of(b, g)[:, n0:n1, :], in_=w_raw[b, g][:, :, n0:n1].rearrange("p j n -> p n j"))

        def quantize_w(b, g):
            w_codes[b, g] = work.tile([P, NB], U32, name="w_codes", bufs=9, align_bytes=64)
            w_scales[b, g] = work.tile([P, NB], U8, name="w_scales", bufs=9, align_bytes=64)
            nc.vector.quantize_mx(
                out=w_codes[b, g][:].bitcast(E4M3),
                scales=w_scales[b, g][:],
                in_=w_grouped[b, g][:].rearrange("p n j -> p (n j)"),
            )

        def mx_pass(b, t, g, h0=0, h1=HB):
            if g == 0:
                acc[b, t, h0] = psum.tile([P, h1 - h0, HD], F32, name="bank")
            nc.tensor.matmul_mx(
                out=acc[b, t, h0][:].rearrange("p h c -> p (h c)"),
                lhsT=x_codes[t][:, g, :].bitcast(E5M2),
                lhsT_scale=x_scales[t][:, g, :],
                rhs=w_codes[b, g][:, h0 * HD : h1 * HD].bitcast(E4M3),
                rhs_scale=w_scales[b, g][:, h0 * HD : h1 * HD],
                start=(g == 0),
                stop=(g == PASSES - 1),
            )

        def mx_unit(b, t, h0=0, h1=HB):
            for g in range(PASSES):
                mx_pass(b, t, g, h0, h1)

        def head_stats(b, t):
            stats[b, t] = work.tile([P, HB, 3], F32, name="stats", bufs=3)
            for h in range(0, HB, 2):
                nc.vector.bn_stats(
                    out=stats[b, t][:, h : h + 2, :].rearrange("p h s -> p (h s)"),
                    in_=acc[b, t, 0][:, h : h + 2, :].rearrange("p h c -> p c h"),
                )

        def inverse_std(b, t):
            rstd[b, t] = work.tile([P, HB], F32, name="rstd", bufs=3)
            nc.scalar.activation(
                out=rstd[b, t][:], in_=stats[b, t][:, :, 2], func=ACT.Abs_reciprocal_sqrt, scale=1.0 / HD, bias=EPS
            )

        def norm_bias(b, t):
            neg_mean = work.tile([P, HB], F32, name="neg_mean", bufs=3)
            nmr[b, t] = work.tile([P, HB], F32, name="nmr", bufs=3)
            if not NMR_G:
                return nc.vector.scalar_tensor_tensor(out=nmr[b, t][:], in0=stats[b, t][:, :, 1], scalar=-1.0, in1=rstd[b, t][:], op0=ALU.mult, op1=ALU.mult)
            nc.gpsimd.tensor_scalar(
                out=neg_mean[:], in0=stats[b, t][:, :, 1], scalar1=-1.0, scalar2=0.0, op0=ALU.mult, op1=ALU.add
            )
            nc.gpsimd.tensor_tensor(out=nmr[b, t][:], in0=neg_mean[:], in1=rstd[b, t][:], op=ALU.mult)

        def normalize(b, t):
            normed[b, t] = work.tile([P, HB, HD], F32, name="normed", bufs=3)
            for h in range(HB):
                nc.scalar.activation(
                    out=normed[b, t][:, h, :],
                    in_=acc[b, t, 0][:, h, :],
                    func=ACT.Identity,
                    scale=rstd[b, t][:, h : h + 1],
                    bias=nmr[b, t][:, h : h + 1],
                )

        def transpose_normed(b, t):
            normed_t[b, t] = psum.tile([P, HB, P], F32, name="bank")
            for h in range(HB):
                nc.tensor.transpose(normed_t[b, t][:, h, :], normed[b, t][:, h, :], ident[:])

        def products(b, t):
            prods[b, t] = work.tile([P, HB, 2, P], F32, name="prods", bufs=2)
            nc.vector.tensor_tensor(
                out=prods[b, t][:],
                in0=normed_t[b, t][:].unsqueeze(2).to_broadcast([P, HB, 2, P]),
                in1=gain[b > 0][:, t, :, :].unsqueeze(1).to_broadcast([P, HB, 2, P]),
                op=ALU.mult,
            )

        def sum_back(b, t):
            res[b, t] = psum.tile([P, HB, HD], F32, name="bank")
            for h in range(HB):
                terms = ((shift[b > 0][:, t, :], ident), (prods[b, t][:, h, 0, :], ident), (prods[b, t][:, h, 1, :], swap))
                for i, (term, perm) in enumerate(terms):
                    nc.tensor.matmul(
                        res[b, t][:, h, :], lhsT=term, rhs=perm[:], is_transpose=True, start=(i == 0), stop=(i == 2)
                    )

        def copy_out(b, t, bank, copy, h0=0, h1=HB):
            out, head0 = blocks[b][2], blocks[b][3]
            stage = work.tile([P, h1 - h0, HD], F32, name="stage", bufs=6)
            copy(out=stage[:], in_=bank[:])
            rows = out[0, head0 + h0 : head0 + h1].rearrange("h (p t) c -> p h t c", t=TT)
            nc.sync.dma_start(out=rows[:, :, t, :], in_=stage[:])

        gain, shift = {}, {}

        def build_tables(is_q):
            c0 = 0 if is_q else 1
            gain[is_q] = keep.tile([P, TT, 2, P], F32, name="gain%d" % c0)
            shift[is_q] = keep.tile([P, TT, P], F32, name="shift%d" % c0)
            beta_cos = work.tile([P, TT, P], F32, name="normed", bufs=3)
            nc.vector.tensor_scalar(
                out=beta_cos[:], in0=cs_t[:, :, 0, :], scalar1=cols[:, 2 + c0 : 3 + c0], scalar2=None, op0=ALU.mult
            )
            if GAIN_S & (2 if is_q else 1):
                nc.scalar.activation(out=gain[is_q][:], in_=cs_t[:], func=ACT.Identity, scale=cols[:, c0 : c0 + 1])
            else:
                nc.vector.tensor_scalar(
                    out=gain[is_q][:], in0=cs_t[:], scalar1=cols[:, c0 : c0 + 1], scalar2=None, op0=ALU.mult
                )
            nc.vector.scalar_tensor_tensor(
                out=shift[is_q][:], in0=sin_t[:], scalar=cols[:, 6 + c0 : 7 + c0], in1=beta_cos[:], op0=ALU.mult, op1=ALU.add
            )

        if XFIRST:
            transpose_x(0)
        nc.vector.tensor_copy(out=cs[:, :, 1, 0:HALF], in_=sin_sb[:, :, HALF:HD])
        nc.vector.tensor_scalar(out=cs[:, :, 1, HALF:HD], in0=sin_sb[:, :, 0:HALF], scalar1=-1.0, scalar2=None, op0=ALU.mult)
        nc.vector.tensor_scalar(out=vec_rows[:, 1, 0:HALF], in0=vec_rows[:, 0, HALF:HD], scalar1=-1.0, scalar2=None, op0=ALU.mult)
        nc.vector.tensor_copy(out=vec_rows[:, 1, HALF:HD], in_=vec_rows[:, 0, 0:HALF])
        cs_bank = psum.tile([P, TT, 2, P], BF16, name="bank")
        sin_bank = psum.tile([P, TT + 2, P], BF16, name="bank")
        for t in range(TT):
            for r in range(2):
                nc.tensor.transpose(cs_bank[:, t, r, :], cs[:, t, r, :], ident_bf[:])
        for t in range(TT):
            nc.tensor.transpose(sin_bank[:, t, :], sin_sb[:, t, :], ident_bf[:])
        for r in range(2):
            nc.tensor.transpose(sin_bank[:, TT + r, :], vec_rows[:, r, :], ident_bf[:])
        if not XFIRST:
            transpose_x(0)
        cols3 = keep.tile([P, 2, 4], F32, name="cols")
        cols = cols3[:].rearrange("p r v -> p (r v)")
        sin_t = keep.tile([P, TT, P], BF16, name="sin_t")
        cs_t = keep.tile([P, TT, 2, P], BF16, name="cs_t")
        nc.vector.tensor_copy(out=cs_t[:], in_=cs_bank[:])
        nc.vector.tensor_copy(out=sin_t[:], in_=sin_bank[:, 0:TT, :])
        nc.vector.tensor_copy(out=cols3[:], in_=sin_bank[:, TT : TT + 2, 0:4])

        if KT == -1:
            build_tables(False)
        interleave_w(0, 0, nc.scalar.copy, 0, NB)
        quantize_x(0)
        interleave_w(0, 1, nc.vector.tensor_copy, 0, NB)
        interleave_w(0, 2, nc.scalar.copy, 0, NB)
        quantize_w(0, 0)
        quantize_w(0, 1)
        interleave_w(0, 3, nc.scalar.copy, 0, HEAD_S)
        interleave_w(0, 3, nc.vector.tensor_copy, HEAD_S, NB)
        transpose_x(1)
        quantize_w(0, 2)
        quantize_w(0, 3)
        if KT == -2:
            build_tables(False)
        if Q_TABLES_AT == -2:
            build_tables(True)
        if TX2:
            transpose_x(2)
        mx_unit(0, 0)
        if not TX2:
            transpose_x(2)
        quantize_x(1)
        transpose_x(3)

        to_interleave = {c: [] for c in range(n_units + 3)}
        to_quantize = {c: [] for c in range(n_units + 3)}
        for b in range(1, n_blocks):
            for g in range(PASSES):
                c, v_cols, g_cols = TT * (b - 1) - 2 + g, V_COLS, G_COLS
                if b == 2 and g < G_FROM:
                    v_cols, g_cols = V_NOG, 0
                if b == 1:
                    c, v_cols, g_cols = (g + 1) // 2, RV[g], 0
                to_interleave[c].append((b, g, v_cols, g_cols))
                to_quantize[min(c + 1, TT * (b - 1) + 2)].append((b, g))

        def unit(c):
            return divmod(c, TT)

        for c in range(n_units + 3):
            if c + 1 < n_units:
                mx_unit(*unit(c + 1))
            for g in range(PASSES):
                if min(n_units - 3 + g, n_units - 1) == c if VEARLY else c == n_units - 1:
                    mx_pass(v_block, 0, g)
            for wb, wg, v_cols, g_cols in to_interleave[c]:
                interleave_w_gpsimd(wb, wg, NB - g_cols, NB)
            if c < n_units:
                head_stats(*unit(c))
                inverse_std(*unit(c))
                if NMR_G:
                    norm_bias(*unit(c))
            if 0 <= c - 1 < n_units:
                transpose_normed(*unit(c - 1))
            if c + 1 == n_units:
                mx_unit(v_block, 1)
            if 0 <= c - 2 < n_units:
                products(*unit(c - 2))
                sum_back(*unit(c - 2))
            if c == n_units:
                mx_unit(v_block, 2)
            if c == n_units + 1:
                mx_unit(v_block, 3, 0, HB // 2)
                mx_unit(v_block, 3, HB // 2, HB)
            if c + 2 < TT:
                quantize_x(c + 2)
            if c == KT:
                build_tables(False)
            if c < n_units and not NMR_G:
                norm_bias(*unit(c))
            for wb, wg, v_cols, g_cols in to_interleave[c]:
                interleave_w(wb, wg, nc.vector.tensor_copy, 0, v_cols)
                interleave_w(wb, wg, nc.scalar.copy, v_cols, NB - g_cols)
            if c == n_units - 1:
                normalize(*unit(c))
            if 0 <= c - 3 < n_units:
                copy_out(*unit(c - 3), res[unit(c - 3)], nc.scalar.copy)
            if c < n_units - 1:
                normalize(*unit(c))
            for wb, wg in to_quantize[c]:
                quantize_w(wb, wg)
            if c == Q_TABLES_AT:
                build_tables(True)
            if c == n_units - 1:
                copy_out(v_block, 0, acc[v_block, 0, 0], nc.scalar.copy)
            if n_units <= c < n_units + 2:
                copy_out(v_block, c - n_units + 1, acc[v_block, c - n_units + 1, 0], nc.vector.tensor_copy)
            if c == n_units + 2:
                copy_out(v_block, 3, acc[v_block, 3, 0], nc.vector.tensor_copy, 0, HB // 2)
                copy_out(v_block, 3, acc[v_block, 3, HB // 2], nc.scalar.copy, HB // 2, HB)
